import numpy as np
import ml_dtypes


def mxq(x, axis, fmt="e4m3"):
    dtype, down = {"e4m3": (ml_dtypes.float8_e4m3fn, 7), "e5m2": (ml_dtypes.float8_e5m2, 14)}[fmt]
    v = np.moveaxis(np.asarray(x, np.float32).astype(ml_dtypes.bfloat16).astype(np.float64), axis, -1)
    blocks = v.reshape(v.shape[:-1] + (-1, 32))
    amax = np.abs(blocks).max(-1, keepdims=True)
    byte = np.maximum(np.where(amax > 0, np.frexp(amax)[1] - 1 + 127, 0) - down, 1)
    scale = np.exp2(byte - 127.0)
    codes = (blocks / scale).astype(np.float32).astype(dtype).astype(np.float64)
    return np.moveaxis((codes * scale).reshape(v.shape), -1, axis)


WIDE = False


def mx_kscale(k):
    if not WIDE:
        return np.ones(k)
    levels = np.array([10, -10, 5, -5, 0])
    a = np.random.permutation(np.resize(levels, k // 512 * 4)).reshape(k // 512, 4)
    idx = np.arange(k)
    return np.exp2(a[idx // 512, idx % 128 // 32])


BF16 = ml_dtypes.bfloat16


def bf(x):
    return np.asarray(x, np.float32).astype(BF16)


def f64(x):
    return np.asarray(x).astype(np.float64)


B, I, H, L, P, G = 128, 1024, 1024, 4, 2, 4


def sigmoid(v):
    return 1.0 / (1.0 + np.exp(-v))


def setup_inputs():
    s = mx_kscale(I)
    return {"h_below": bf(np.random.standard_normal((B, I)) * 0.3 * s),
            "gates_rec": bf(np.random.standard_normal((B, G * H)) * 0.7),
            "c": bf(np.random.standard_normal((B, H))),
            "w_ih": bf(np.random.standard_normal((G * H, I)) * 1.5 / np.sqrt(I) / s),
            "b_ih": bf(np.random.standard_normal(G * H) * 0.3),
            "b_hh": bf(np.random.standard_normal(G * H) * 0.3)}


def reference(h_below, gates_rec, c, w_ih, b_ih, b_hh):
    gates = (mxq(f64(h_below), 1, "e4m3") @ mxq(f64(w_ih), 1, "e4m3").T) + f64(b_ih) + f64(gates_rec) + f64(b_hh)
    i, f, g, o = np.split(gates, G, axis=-1)
    c_new = sigmoid(f) * f64(c) + sigmoid(i) * np.tanh(g)
    h_new = sigmoid(o) * np.tanh(c_new)
    return h_new, c_new

@@ -1,0 +1,234 @@
+from contextlib import ExitStack
+
+import concourse.mybir as mybir
+from concourse.masks import make_identity
+
+F32 = mybir.dt.float32
+BF16 = mybir.dt.bfloat16
+U32 = mybir.dt.uint32
+U8 = mybir.dt.uint8
+FP8X4 = mybir.dt.float8_e4m3fn_x4
+ACT = mybir.ActivationFunctionType
+ALU = mybir.AluOpType
+
+P = 128
+FEATURES = 1024
+HIDDEN = 1024
+GATES = 4
+PACK = 4
+PASSES = FEATURES // (P * PACK)
+HALVES = 2
+WORDS = FEATURES // 2
+CHUNKS = HIDDEN // P
+BANK = 512
+PAIR = 2
+STORE_CHUNKS = 2
+
+FLOPS = 2 * P * FEATURES * GATES * HIDDEN
+
+
+def tile_yourlstm_pc_kernel(tc, h_below, gates_rec, c_old, w_ih, b_ih, b_hh, out_0, out_1):
+    nc = tc.nc
+    with ExitStack() as ctx:
+        keep = ctx.enter_context(tc.tile_pool(name="keep", bufs=1))
+        w_pool = ctx.enter_context(tc.tile_pool(name="w", bufs=CHUNKS))
+        stage = ctx.enter_context(tc.tile_pool(name="stage", bufs=3))
+        psum_words = ctx.enter_context(tc.psum_pool(name="psum_words", bufs=4))
+        psum_gates = ctx.enter_context(tc.psum_pool(name="psum_gates", bufs=2))
+        psum_bias = ctx.enter_context(tc.psum_pool(name="psum_bias", bufs=2))
+
+        bias_rows = keep.tile([P, P], BF16)
+        nc.vector.memset(bias_rows[:], 0.0)
+        bias_blocks = GATES * CHUNKS
+        nc.sync.dma_start(out=bias_rows[0:bias_blocks, :], in_=b_ih.rearrange("(m r) -> m r", r=P))
+        nc.sync.dma_start(
+            out=bias_rows[bias_blocks : 2 * bias_blocks, :], in_=b_hh.rearrange("(m r) -> m r", r=P)
+        )
+        h_rows = keep.tile([P, FEATURES], BF16)
+        nc.sync.dma_start(out=h_rows[:], in_=h_below)
+
+        w_chunks = w_ih.rearrange("(g j r) k -> j r g k", g=GATES, r=P)
+        w_rows = []
+
+        def load_w(j):
+            w_tile = w_pool.tile([P, GATES * FEATURES], BF16, name="w_tile", tag="w_tile")
+            nc.sync.dma_start(out=w_tile[:].rearrange("r (g k) -> r g k", g=GATES), in_=w_chunks[j])
+            w_rows.append(w_tile)
+
+        load_w(0)
+        rec_rows = keep.tile([P, GATES * HIDDEN], BF16)
+        nc.sync.dma_start(out=rec_rows[:], in_=gates_rec)
+        c_rows = keep.tile([P, HIDDEN], BF16)
+        nc.sync.dma_start(out=c_rows[:], in_=c_old)
+        for j in range(1, CHUNKS):
+            load_w(j)
+
+        ident_f32 = keep.tile([P, P], F32)
+        make_identity(nc, ident_f32[:])
+        ident_bf16 = keep.tile([P, P], BF16)
+        nc.vector.tensor_copy(out=ident_bf16[:], in_=ident_f32[:])
+        warm = keep.tile([P, 1], F32)
+        nc.vector.memset(warm[:], 0.0)
+        warm_out = keep.tile([P, 1], F32)
+        nc.scalar.activation(out=warm_out[:], in_=warm[:], func=ACT.Sigmoid)
+
+        bias_t = psum_bias.tile([P, P], BF16, tag="bias_bank")
+        nc.tensor.transpose(bias_t[:], bias_rows[:], ident_bf16[:])
+        bias_both = keep.tile([P, 2 * bias_blocks], F32)
+        nc.vector.tensor_copy(out=bias_both[:], in_=bias_t[:, 0 : 2 * bias_blocks])
+        bias_col = keep.tile([P, bias_blocks], F32)
+        nc.vector.tensor_add(
+            out=bias_col[:], in0=bias_both[:, 0:bias_blocks], in1=bias_both[:, bias_blocks : 2 * bias_blocks]
+        )
+
+        h_words = h_rows[:].bitcast(F32)
+        h_t = psum_bias.tile([P, PASSES, HALVES, P], F32, tag="bias_bank")
+        for s in range(PASSES):
+            for u in range(HALVES):
+                first = (s * HALVES + u) * P
+                nc.tensor.transpose(h_t[:, s, u, :], h_words[:, first : first + P], ident_f32[:])
+        h_grouped = keep.tile([P, PASSES * P * PACK], BF16, align_bytes=64)
+        nc.vector.tensor_copy(
+            out=h_grouped[:].bitcast(F32).rearrange("q (s m u) -> q s m u", s=PASSES, u=HALVES),
+            in_=h_t[:].rearrange("q s u m -> q s m u"),
+        )
+        h_codes = keep.tile([P, PASSES * P], U32, align_bytes=64)
+        h_scales = keep.tile([P, PASSES * P], U8, align_bytes=64)
+        nc.vector.quantize_mx(out=h_codes[:].bitcast(FP8X4), scales=h_scales[:], in_=h_grouped[:])
+
+        rec_view = rec_rows[:].rearrange("b (g j r) -> b j g r", g=GATES, r=P)
+        rest = keep.tile([P, CHUNKS, GATES, P], F32)
+        c_new = keep.tile([P, HIDDEN], F32)
+        h_new = keep.tile([P, HIDDEN], F32)
+        bias_banks = {}
+        word_banks = {}
+        grouped = {}
+        codes = {}
+        scales = {}
+        products = {}
+        gates = {}
+        sig_if = {}
+        tanh_g = {}
+        sig_o = {}
+        tanh_c = {}
+
+        def live(j):
+            return 0 <= j < CHUNKS
+
+        def units(j):
+            return slice(j * P, (j + 1) * P)
+
+        def broadcast_bias(j):
+            bias_banks[j] = psum_bias.tile([P, GATES, P], F32, name="bias_bank", tag="bias_bank")
+            for g in range(GATES):
+                m = g * CHUNKS + j
+                nc.tensor.transpose(
+                    bias_banks[j][:, g, :], bias_col[:, m : m + 1].to_broadcast([P, P]), ident_f32[:]
+                )
+
+        def add_bias_to_rec(j):
+            nc.vector.tensor_tensor(out=rest[:, j, :, :], in0=bias_banks[j][:], in1=rec_view[:, j, :, :], op=ALU.add)
+
+        def transpose_w(j):
+            words = w_rows[j][:].bitcast(F32)
+            for s in range(PASSES):
+                for pair in range(GATES // PAIR):
+                    bank = psum_words.tile([P, PAIR, HALVES, P], F32, name="word_bank", tag="word_bank")
+                    for g2 in range(PAIR):
+                        for u in range(HALVES):
+                            first = (pair * PAIR + g2) * WORDS + (s * HALVES + u) * P
+                            nc.tensor.transpose(bank[:, g2, u, :], words[:, first : first + P], ident_f32[:])
+                    word_banks[(j, s, pair)] = bank
+            grouped[j] = stage.tile([P, PASSES * BANK * PACK], BF16, name="grouped", tag="grouped", align_bytes=64)
+            codes[j] = stage.tile([P, PASSES * BANK], U32, name="codes", tag="codes", align_bytes=64)
+            scales[j] = stage.tile([P, PASSES * BANK], U8, name="scales", tag="scales", align_bytes=64)
+
+        def regroup(j, s):
+            words = grouped[j][:].bitcast(F32)
+            for pair in range(GATES // PAIR):
+                first = (s * GATES + pair * PAIR) * P * HALVES
+                nc.scalar.copy(
+                    out=words[:, first : first + BANK].rearrange("q (g r u) -> q g r u", g=PAIR, u=HALVES),
+                    in_=word_banks[(j, s, pair)][:].rearrange("q g u r -> q g r u"),
+                )
+
+        def quantise(j, s):
+            nc.vector.quantize_mx(
+                out=codes[j][:, s * BANK : (s + 1) * BANK].bitcast(FP8X4),
+                scales=scales[j][:, s * BANK : (s + 1) * BANK],
+                in_=grouped[j][:, s * BANK * PACK : (s + 1) * BANK * PACK],
+            )
+
+        def multiply(j):
+            products[j] = psum_gates.tile([P, BANK], F32, name="product", tag="product")
+            for s in range(PASSES):
+                nc.tensor.matmul_mx(
+                    out=products[j][:],
+                    lhsT=h_codes[:, s * P : (s + 1) * P].bitcast(FP8X4),
+                    lhsT_scale=h_scales[:, s * P : (s + 1) * P],
+                    rhs=codes[j][:, s * BANK : (s + 1) * BANK].bitcast(FP8X4),
+                    rhs_scale=scales[j][:, s * BANK : (s + 1) * BANK],
+                    start=(s == 0),
+                    stop=(s == PASSES - 1),
+                )
+
+        def add_rest(j):
+            gates[j] = stage.tile([P, GATES, P], F32, name="gates", tag="gates")
+            nc.vector.tensor_tensor(
+                out=gates[j][:].rearrange("b g r -> b (g r)"),
+                in0=products[j][:],
+                in1=rest[:, j, :, :].rearrange("b g r -> b (g r)"),
+                op=ALU.add,
+            )
+
+        def activate_i_f_g(j):
+            sig_if[j] = stage.tile([P, 2, P], F32, name="sig_if", tag="sig_if")
+            nc.scalar.activation(out=sig_if[j][:], in_=gates[j][:, 0:2, :], func=ACT.Sigmoid)
+            tanh_g[j] = stage.tile([P, P], F32, name="tanh_g", tag="tanh_g")
+            nc.scalar.activation(out=tanh_g[j][:], in_=gates[j][:, 2, :], func=ACT.Tanh)
+
+        def update_cell(j):
+            kept = stage.tile([P, P], F32, name="kept", tag="kept")
+            nc.vector.tensor_mul(out=kept[:], in0=sig_if[j][:, 1, :], in1=c_rows[:, units(j)])
+            fresh = stage.tile([P, P], F32, name="fresh", tag="fresh")
+            nc.vector.tensor_mul(out=fresh[:], in0=sig_if[j][:, 0, :], in1=tanh_g[j][:])
+            nc.vector.tensor_add(out=c_new[:, units(j)], in0=kept[:], in1=fresh[:])
+
+        def activate_o_c(j):
+            sig_o[j] = stage.tile([P, P], F32, name="sig_o", tag="sig_o")
+            nc.scalar.activation(out=sig_o[j][:], in_=gates[j][:, 3, :], func=ACT.Sigmoid)
+            tanh_c[j] = stage.tile([P, P], F32, name="tanh_c", tag="tanh_c")
+            nc.scalar.activation(out=tanh_c[j][:], in_=c_new[:, units(j)], func=ACT.Tanh)
+
+        def update_hidden_and_store(j):
+            nc.vector.tensor_mul(out=h_new[:, units(j)], in0=sig_o[j][:], in1=tanh_c[j][:])
+            if (j + 1) % STORE_CHUNKS == 0:
+                cols = slice((j + 1 - STORE_CHUNKS) * P, (j + 1) * P)
+                nc.sync.dma_start(out=out_1[:, cols], in_=c_new[:, cols])
+                nc.sync.dma_start(out=out_0[:, cols], in_=h_new[:, cols])
+
+        for t in range(CHUNKS + 2):
+            if live(t):
+                broadcast_bias(t)
+                transpose_w(t)
+            if live(t - 1):
+                multiply(t - 1)
+            if live(t - 2):
+                activate_i_f_g(t - 2)
+            if live(t):
+                add_bias_to_rec(t)
+            if live(t - 2):
+                update_cell(t - 2)
+            if live(t):
+                regroup(t, 0)
+            if live(t - 2):
+                activate_o_c(t - 2)
+            if live(t - 1):
+                add_rest(t - 1)
+            if live(t):
+                quantise(t, 0)
+            if live(t - 2):
+                update_hidden_and_store(t - 2)
+            if live(t):
+                regroup(t, 1)
+                quantise(t, 1)

@@ -22,6 +22,9 @@ WORDS = FEATURES // 2
 CHUNKS = HIDDEN // P
 BANK = 512
 PAIR = 2
+PAIRS = GATES // PAIR
+REC_PARTS = 2
+REC_CHUNKS = CHUNKS // REC_PARTS
 STORE_CHUNKS = 2
 
 FLOPS = 2 * P * FEATURES * GATES * HIDDEN
@@ -31,37 +34,42 @@ def tile_yourlstm_pc_kernel(tc, h_below, gates_rec, c_old, w_ih, b_ih, b_hh, out
     nc = tc.nc
     with ExitStack() as ctx:
         keep = ctx.enter_context(tc.tile_pool(name="keep", bufs=1))
-        w_pool = ctx.enter_context(tc.tile_pool(name="w", bufs=CHUNKS))
+        w_pool = ctx.enter_context(tc.tile_pool(name="w", bufs=CHUNKS * PAIRS))
+        quant = ctx.enter_context(tc.tile_pool(name="quant", bufs=2 * PAIRS))
         stage = ctx.enter_context(tc.tile_pool(name="stage", bufs=3))
-        psum_words = ctx.enter_context(tc.psum_pool(name="psum_words", bufs=4))
+        psum_words = ctx.enter_context(tc.psum_pool(name="psum_words", bufs=PAIRS * PASSES))
         psum_gates = ctx.enter_context(tc.psum_pool(name="psum_gates", bufs=2))
         psum_bias = ctx.enter_context(tc.psum_pool(name="psum_bias", bufs=2))
+        ctx.enter_context(tc.manual_schedule())
 
-        bias_rows = keep.tile([P, P], BF16)
-        nc.vector.memset(bias_rows[:], 0.0)
         bias_blocks = GATES * CHUNKS
-        nc.sync.dma_start(out=bias_rows[0:bias_blocks, :], in_=b_ih.rearrange("(m r) -> m r", r=P))
-        nc.sync.dma_start(
+        bias_rows = keep.tile([P, P], BF16)
+        nc.vector.memset(bias_rows[2 * bias_blocks : P, :], 0.0)
+        nc.scalar.dma_start(out=bias_rows[0:bias_blocks, :], in_=b_ih.rearrange("(m r) -> m r", r=P))
+        nc.scalar.dma_start(
             out=bias_rows[bias_blocks : 2 * bias_blocks, :], in_=b_hh.rearrange("(m r) -> m r", r=P)
         )
+
         h_rows = keep.tile([P, FEATURES], BF16)
         nc.sync.dma_start(out=h_rows[:], in_=h_below)
-
         w_chunks = w_ih.rearrange("(g j r) k -> j r g k", g=GATES, r=P)
-        w_rows = []
-
-        def load_w(j):
-            w_tile = w_pool.tile([P, GATES * FEATURES], BF16, name="w_tile", tag="w_tile")
-            nc.sync.dma_start(out=w_tile[:].rearrange("r (g k) -> r g k", g=GATES), in_=w_chunks[j])
-            w_rows.append(w_tile)
-
-        load_w(0)
-        rec_rows = keep.tile([P, GATES * HIDDEN], BF16)
-        nc.sync.dma_start(out=rec_rows[:], in_=gates_rec)
+        rec_parts = gates_rec.rearrange("b (g v x) -> v b g x", g=GATES, v=REC_PARTS)
+        w_rows = {}
+        rec_rows = {}
         c_rows = keep.tile([P, HIDDEN], BF16)
-        nc.sync.dma_start(out=c_rows[:], in_=c_old)
-        for j in range(1, CHUNKS):
-            load_w(j)
+        for j in range(CHUNKS):
+            for pair in range(PAIRS):
+                w_rows[(j, pair)] = w_pool.tile([P, PAIR * FEATURES], BF16, name="w_rows", tag="w_rows")
+                nc.sync.dma_start(
+                    out=w_rows[(j, pair)][:].rearrange("r (g k) -> r g k", g=PAIR),
+                    in_=w_chunks[j][:, pair * PAIR : (pair + 1) * PAIR, :],
+                )
+            if j % REC_CHUNKS == 1:
+                v = j // REC_CHUNKS
+                rec_rows[v] = keep.tile([P, GATES, REC_CHUNKS * P], BF16, name="rec_rows%d" % v)
+                nc.sync.dma_start(out=rec_rows[v][:], in_=rec_parts[v])
+            if j == 2:
+                nc.sync.dma_start(out=c_rows[:], in_=c_old)
 
         ident_f32 = keep.tile([P, P], F32)
         make_identity(nc, ident_f32[:])
@@ -71,15 +79,6 @@ def tile_yourlstm_pc_kernel(tc, h_below, gates_rec, c_old, w_ih, b_ih, b_hh, out
         nc.vector.memset(warm[:], 0.0)
         warm_out = keep.tile([P, 1], F32)
         nc.scalar.activation(out=warm_out[:], in_=warm[:], func=ACT.Sigmoid)
-
-        bias_t = psum_bias.tile([P, P], BF16, tag="bias_bank")
-        nc.tensor.transpose(bias_t[:], bias_rows[:], ident_bf16[:])
-        bias_both = keep.tile([P, 2 * bias_blocks], F32)
-        nc.vector.tensor_copy(out=bias_both[:], in_=bias_t[:, 0 : 2 * bias_blocks])
-        bias_col = keep.tile([P, bias_blocks], F32)
-        nc.vector.tensor_add(
-            out=bias_col[:], in0=bias_both[:, 0:bias_blocks], in1=bias_both[:, bias_blocks : 2 * bias_blocks]
-        )
 
         h_words = h_rows[:].bitcast(F32)
         h_t = psum_bias.tile([P, PASSES, HALVES, P], F32, tag="bias_bank")
@@ -92,15 +91,24 @@ def tile_yourlstm_pc_kernel(tc, h_below, gates_rec, c_old, w_ih, b_ih, b_hh, out
             out=h_grouped[:].bitcast(F32).rearrange("q (s m u) -> q s m u", s=PASSES, u=HALVES),
             in_=h_t[:].rearrange("q s u m -> q s m u"),
         )
+
+        bias_t = psum_bias.tile([P, P], BF16, tag="bias_bank")
+        nc.tensor.transpose(bias_t[:], bias_rows[:], ident_bf16[:])
+        bias_both = keep.tile([P, 2 * bias_blocks], F32)
+        nc.vector.tensor_copy(out=bias_both[:], in_=bias_t[:, 0 : 2 * bias_blocks])
+        bias_col = keep.tile([P, bias_blocks], F32)
+        nc.vector.tensor_add(
+            out=bias_col[:], in0=bias_both[:, 0:bias_blocks], in1=bias_both[:, bias_blocks : 2 * bias_blocks]
+        )
+
         h_codes = keep.tile([P, PASSES * P], U32, align_bytes=64)
         h_scales = keep.tile([P, PASSES * P], U8, align_bytes=64)
         nc.vector.quantize_mx(out=h_codes[:].bitcast(FP8X4), scales=h_scales[:], in_=h_grouped[:])
 
-        rec_view = rec_rows[:].rearrange("b (g j r) -> b j g r", g=GATES, r=P)
-        rest = keep.tile([P, CHUNKS, GATES, P], F32)
         c_new = keep.tile([P, HIDDEN], F32)
         h_new = keep.tile([P, HIDDEN], F32)
         bias_banks = {}
+        rest = {}
         word_banks = {}
         grouped = {}
         codes = {}
@@ -127,57 +135,64 @@ def tile_yourlstm_pc_kernel(tc, h_below, gates_rec, c_old, w_ih, b_ih, b_hh, out
                 )
 
         def add_bias_to_rec(j):
-            nc.vector.tensor_tensor(out=rest[:, j, :, :], in0=bias_banks[j][:], in1=rec_view[:, j, :, :], op=ALU.add)
+            rest[j] = stage.tile([P, GATES, P], F32, name="rest", tag="rest")
+            nc.vector.tensor_tensor(
+                out=rest[j][:],
+                in0=bias_banks[j][:],
+                in1=rec_rows[j // REC_CHUNKS][:, :, units(j % REC_CHUNKS)],
+                op=ALU.add,
+            )
 
         def transpose_w(j):
-            words = w_rows[j][:].bitcast(F32)
-            for s in range(PASSES):
-                for pair in range(GATES // PAIR):
+            for pair in range(PAIRS):
+                words = w_rows[(j, pair)][:].bitcast(F32)
+                for s in range(PASSES):
                     bank = psum_words.tile([P, PAIR, HALVES, P], F32, name="word_bank", tag="word_bank")
                     for g2 in range(PAIR):
                         for u in range(HALVES):
-                            first = (pair * PAIR + g2) * WORDS + (s * HALVES + u) * P
+                            first = g2 * WORDS + (s * HALVES + u) * P
                             nc.tensor.transpose(bank[:, g2, u, :], words[:, first : first + P], ident_f32[:])
-                    word_banks[(j, s, pair)] = bank
-            grouped[j] = stage.tile([P, PASSES * BANK * PACK], BF16, name="grouped", tag="grouped", align_bytes=64)
-            codes[j] = stage.tile([P, PASSES * BANK], U32, name="codes", tag="codes", align_bytes=64)
-            scales[j] = stage.tile([P, PASSES * BANK], U8, name="scales", tag="scales", align_bytes=64)
+                    word_banks[(j, pair, s)] = bank
 
-        def regroup(j, s):
-            words = grouped[j][:].bitcast(F32)
-            for pair in range(GATES // PAIR):
-                first = (s * GATES + pair * PAIR) * P * HALVES
+        def regroup(j, pair):
+            grouped[(j, pair)] = quant.tile(
+                [P, PASSES * PAIR * P * PACK], BF16, name="grouped", tag="grouped", align_bytes=64
+            )
+            words = grouped[(j, pair)][:].bitcast(F32)
+            for s in range(PASSES):
                 nc.scalar.copy(
-                    out=words[:, first : first + BANK].rearrange("q (g r u) -> q g r u", g=PAIR, u=HALVES),
-                    in_=word_banks[(j, s, pair)][:].rearrange("q g u r -> q g r u"),
+                    out=words[:, s * BANK : (s + 1) * BANK].rearrange("q (g r u) -> q g r u", g=PAIR, u=HALVES),
+                    in_=word_banks[(j, pair, s)][:].rearrange("q g u r -> q g r u"),
                 )
 
-        def quantise(j, s):
+        def quantise(j, pair):
+            codes[(j, pair)] = quant.tile([P, PASSES * PAIR * P], U32, name="codes", tag="codes", align_bytes=64)
+            scales[(j, pair)] = quant.tile([P, PASSES * PAIR * P], U8, name="scales", tag="scales", align_bytes=64)
             nc.vector.quantize_mx(
-                out=codes[j][:, s * BANK : (s + 1) * BANK].bitcast(FP8X4),
-                scales=scales[j][:, s * BANK : (s + 1) * BANK],
-                in_=grouped[j][:, s * BANK * PACK : (s + 1) * BANK * PACK],
+                out=codes[(j, pair)][:].bitcast(FP8X4), scales=scales[(j, pair)][:], in_=grouped[(j, pair)][:]
             )
 
         def multiply(j):
-            products[j] = psum_gates.tile([P, BANK], F32, name="product", tag="product")
-            for s in range(PASSES):
-                nc.tensor.matmul_mx(
-                    out=products[j][:],
-                    lhsT=h_codes[:, s * P : (s + 1) * P].bitcast(FP8X4),
-                    lhsT_scale=h_scales[:, s * P : (s + 1) * P],
-                    rhs=codes[j][:, s * BANK : (s + 1) * BANK].bitcast(FP8X4),
-                    rhs_scale=scales[j][:, s * BANK : (s + 1) * BANK],
-                    start=(s == 0),
-                    stop=(s == PASSES - 1),
-                )
+            products[j] = psum_gates.tile([P, GATES * P], F32, name="product", tag="product")
+            width = PAIR * P
+            for pair in range(PAIRS):
+                for s in range(PASSES):
+                    nc.tensor.matmul_mx(
+                        out=products[j][:, pair * width : (pair + 1) * width],
+                        lhsT=h_codes[:, s * P : (s + 1) * P].bitcast(FP8X4),
+                        lhsT_scale=h_scales[:, s * P : (s + 1) * P],
+                        rhs=codes[(j, pair)][:, s * width : (s + 1) * width].bitcast(FP8X4),
+                        rhs_scale=scales[(j, pair)][:, s * width : (s + 1) * width],
+                        start=(s == 0),
+                        stop=(s == PASSES - 1),
+                    )
 
         def add_rest(j):
             gates[j] = stage.tile([P, GATES, P], F32, name="gates", tag="gates")
             nc.vector.tensor_tensor(
                 out=gates[j][:].rearrange("b g r -> b (g r)"),
                 in0=products[j][:],
-                in1=rest[:, j, :, :].rearrange("b g r -> b (g r)"),
+                in1=rest[j][:].rearrange("b g r -> b (g r)"),
                 op=ALU.add,
             )
 
@@ -187,12 +202,18 @@ def tile_yourlstm_pc_kernel(tc, h_below, gates_rec, c_old, w_ih, b_ih, b_hh, out
             tanh_g[j] = stage.tile([P, P], F32, name="tanh_g", tag="tanh_g")
             nc.scalar.activation(out=tanh_g[j][:], in_=gates[j][:, 2, :], func=ACT.Tanh)
 
+        def store(out, result, j):
+            if (j + 1) % STORE_CHUNKS == 0:
+                cols = slice((j + 1 - STORE_CHUNKS) * P, (j + 1) * P)
+                nc.sync.dma_start(out=out[:, cols], in_=result[:, cols])
+
         def update_cell(j):
             kept = stage.tile([P, P], F32, name="kept", tag="kept")
             nc.vector.tensor_mul(out=kept[:], in0=sig_if[j][:, 1, :], in1=c_rows[:, units(j)])
             fresh = stage.tile([P, P], F32, name="fresh", tag="fresh")
             nc.vector.tensor_mul(out=fresh[:], in0=sig_if[j][:, 0, :], in1=tanh_g[j][:])
             nc.vector.tensor_add(out=c_new[:, units(j)], in0=kept[:], in1=fresh[:])
+            store(out_1, c_new, j)
 
         def activate_o_c(j):
             sig_o[j] = stage.tile([P, P], F32, name="sig_o", tag="sig_o")
@@ -200,35 +221,32 @@ def tile_yourlstm_pc_kernel(tc, h_below, gates_rec, c_old, w_ih, b_ih, b_hh, out
             tanh_c[j] = stage.tile([P, P], F32, name="tanh_c", tag="tanh_c")
             nc.scalar.activation(out=tanh_c[j][:], in_=c_new[:, units(j)], func=ACT.Tanh)
 
-        def update_hidden_and_store(j):
+        def update_hidden(j):
             nc.vector.tensor_mul(out=h_new[:, units(j)], in0=sig_o[j][:], in1=tanh_c[j][:])
-            if (j + 1) % STORE_CHUNKS == 0:
-                cols = slice((j + 1 - STORE_CHUNKS) * P, (j + 1) * P)
-                nc.sync.dma_start(out=out_1[:, cols], in_=c_new[:, cols])
-                nc.sync.dma_start(out=out_0[:, cols], in_=h_new[:, cols])
+            store(out_0, h_new, j)
 
         for t in range(CHUNKS + 2):
+            if live(t - 1):
+                broadcast_bias(t - 1)
             if live(t):
-                broadcast_bias(t)
                 transpose_w(t)
             if live(t - 1):
                 multiply(t - 1)
             if live(t - 2):
                 activate_i_f_g(t - 2)
-            if live(t):
-                add_bias_to_rec(t)
-            if live(t - 2):
-                update_cell(t - 2)
+            if live(t - 1):
+                add_bias_to_rec(t - 1)
             if live(t):
                 regroup(t, 0)
             if live(t - 2):
+                update_cell(t - 2)
                 activate_o_c(t - 2)
             if live(t - 1):
                 add_rest(t - 1)
             if live(t):
                 quantise(t, 0)
-            if live(t - 2):
-                update_hidden_and_store(t - 2)
-            if live(t):
                 regroup(t, 1)
+            if live(t - 2):
+                update_hidden(t - 2)
+            if live(t):
                 quantise(t, 1)

@@ -37,9 +37,9 @@ def tile_yourlstm_pc_kernel(tc, h_below, gates_rec, c_old, w_ih, b_ih, b_hh, out
         w_pool = ctx.enter_context(tc.tile_pool(name="w", bufs=CHUNKS * PAIRS))
         quant = ctx.enter_context(tc.tile_pool(name="quant", bufs=2 * PAIRS))
         stage = ctx.enter_context(tc.tile_pool(name="stage", bufs=3))
-        psum_words = ctx.enter_context(tc.psum_pool(name="psum_words", bufs=PAIRS * PASSES))
-        psum_gates = ctx.enter_context(tc.psum_pool(name="psum_gates", bufs=2))
-        psum_bias = ctx.enter_context(tc.psum_pool(name="psum_bias", bufs=2))
+        psum_words = ctx.enter_context(tc.psum_pool(name="psum_words", bufs=3 * PASSES))
+        psum_gates = ctx.enter_context(tc.psum_pool(name="psum_gates", bufs=1))
+        psum_bias = ctx.enter_context(tc.psum_pool(name="psum_bias", bufs=1))
         ctx.enter_context(tc.manual_schedule())
 
         bias_blocks = GATES * CHUNKS
@@ -117,6 +117,8 @@ def tile_yourlstm_pc_kernel(tc, h_below, gates_rec, c_old, w_ih, b_ih, b_hh, out
         gates = {}
         sig_if = {}
         tanh_g = {}
+        kept = {}
+        fresh = {}
         sig_o = {}
         tanh_c = {}
 
@@ -207,12 +209,14 @@ def tile_yourlstm_pc_kernel(tc, h_below, gates_rec, c_old, w_ih, b_ih, b_hh, out
                 cols = slice((j + 1 - STORE_CHUNKS) * P, (j + 1) * P)
                 nc.sync.dma_start(out=out[:, cols], in_=result[:, cols])
 
+        def gate_cell(j):
+            kept[j] = stage.tile([P, P], F32, name="kept", tag="kept")
+            nc.vector.tensor_mul(out=kept[j][:], in0=sig_if[j][:, 1, :], in1=c_rows[:, units(j)])
+            fresh[j] = stage.tile([P, P], F32, name="fresh", tag="fresh")
+            nc.vector.tensor_mul(out=fresh[j][:], in0=sig_if[j][:, 0, :], in1=tanh_g[j][:])
+
         def update_cell(j):
-            kept = stage.tile([P, P], F32, name="kept", tag="kept")
-            nc.vector.tensor_mul(out=kept[:], in0=sig_if[j][:, 1, :], in1=c_rows[:, units(j)])
-            fresh = stage.tile([P, P], F32, name="fresh", tag="fresh")
-            nc.vector.tensor_mul(out=fresh[:], in0=sig_if[j][:, 0, :], in1=tanh_g[j][:])
-            nc.vector.tensor_add(out=c_new[:, units(j)], in0=kept[:], in1=fresh[:])
+            nc.vector.tensor_add(out=c_new[:, units(j)], in0=kept[j][:], in1=fresh[j][:])
             store(out_1, c_new, j)
 
         def activate_o_c(j):
@@ -234,6 +238,7 @@ def tile_yourlstm_pc_kernel(tc, h_below, gates_rec, c_old, w_ih, b_ih, b_hh, out
                 multiply(t - 1)
             if live(t - 2):
                 activate_i_f_g(t - 2)
+                gate_cell(t - 2)
             if live(t - 1):
                 add_bias_to_rec(t - 1)
             if live(t):

@@ -15,17 +15,17 @@ P = 128
 FEATURES = 1024
 HIDDEN = 1024
 GATES = 4
+GATE_F, GATE_G, GATE_O = 1, 2, 3
 PACK = 4
 PASSES = FEATURES // (P * PACK)
 HALVES = 2
 WORDS = FEATURES // 2
-CHUNKS = HIDDEN // P
 BANK = 512
-PAIR = 2
-PAIRS = GATES // PAIR
-REC_PARTS = 2
-REC_CHUNKS = CHUNKS // REC_PARTS
-STORE_CHUNKS = 2
+PARTS = HIDDEN // BANK
+SLABS = PARTS * GATES
+PIECES = 2
+ROWS = BANK // PIECES
+TILES = ROWS // P
 
 FLOPS = 2 * P * FEATURES * GATES * HIDDEN
 
@@ -34,15 +34,28 @@ def tile_yourlstm_pc_kernel(tc, h_below, gates_rec, c_old, w_ih, b_ih, b_hh, out
     nc = tc.nc
     with ExitStack() as ctx:
         keep = ctx.enter_context(tc.tile_pool(name="keep", bufs=1))
-        w_pool = ctx.enter_context(tc.tile_pool(name="w", bufs=CHUNKS * PAIRS))
-        quant = ctx.enter_context(tc.tile_pool(name="quant", bufs=2 * PAIRS))
-        stage = ctx.enter_context(tc.tile_pool(name="stage", bufs=3))
+        w_pool = ctx.enter_context(tc.tile_pool(name="w", bufs=SLABS * PIECES))
+        quant = ctx.enter_context(tc.tile_pool(name="quant", bufs=2 * PIECES))
+        stage = ctx.enter_context(tc.tile_pool(name="stage", bufs=2))
+        active_pool = ctx.enter_context(tc.tile_pool(name="active", bufs=GATES))
         psum_words = ctx.enter_context(tc.psum_pool(name="psum_words", bufs=3 * PASSES))
         psum_gates = ctx.enter_context(tc.psum_pool(name="psum_gates", bufs=1))
         psum_bias = ctx.enter_context(tc.psum_pool(name="psum_bias", bufs=1))
         ctx.enter_context(tc.manual_schedule())
 
-        bias_blocks = GATES * CHUNKS
+        def gate_of(t):
+            return t % GATES
+
+        def part_of(t):
+            return t // GATES
+
+        def live(t):
+            return 0 <= t < SLABS
+
+        def units(part):
+            return slice(part * BANK, (part + 1) * BANK)
+
+        bias_blocks = GATES * HIDDEN // P
         bias_rows = keep.tile([P, P], BF16)
         nc.vector.memset(bias_rows[2 * bias_blocks : P, :], 0.0)
         nc.scalar.dma_start(out=bias_rows[0:bias_blocks, :], in_=b_ih.rearrange("(m r) -> m r", r=P))
@@ -52,23 +65,22 @@ def tile_yourlstm_pc_kernel(tc, h_below, gates_rec, c_old, w_ih, b_ih, b_hh, out
 
         h_rows = keep.tile([P, FEATURES], BF16)
         nc.sync.dma_start(out=h_rows[:], in_=h_below)
-        w_chunks = w_ih.rearrange("(g j r) k -> j r g k", g=GATES, r=P)
-        rec_parts = gates_rec.rearrange("b (g v x) -> v b g x", g=GATES, v=REC_PARTS)
+        w_pieces = w_ih.rearrange("(g v e x r) k -> g v e r x k", g=GATES, v=PARTS, e=PIECES, r=P)
+        rec_parts = gates_rec.rearrange("b (g v y) -> v b g y", g=GATES, v=PARTS)
         w_rows = {}
         rec_rows = {}
         c_rows = keep.tile([P, HIDDEN], BF16)
-        for j in range(CHUNKS):
-            for pair in range(PAIRS):
-                w_rows[(j, pair)] = w_pool.tile([P, PAIR * FEATURES], BF16, name="w_rows", tag="w_rows")
+        for t in range(SLABS):
+            for e in range(PIECES):
+                w_rows[(t, e)] = w_pool.tile([P, TILES * FEATURES], BF16, name="w_rows", tag="w_rows")
                 nc.sync.dma_start(
-                    out=w_rows[(j, pair)][:].rearrange("r (g k) -> r g k", g=PAIR),
-                    in_=w_chunks[j][:, pair * PAIR : (pair + 1) * PAIR, :],
+                    out=w_rows[(t, e)][:].rearrange("r (x k) -> r x k", x=TILES),
+                    in_=w_pieces[gate_of(t), part_of(t), e],
                 )
-            if j % REC_CHUNKS == 1:
-                v = j // REC_CHUNKS
-                rec_rows[v] = keep.tile([P, GATES, REC_CHUNKS * P], BF16, name="rec_rows%d" % v)
-                nc.sync.dma_start(out=rec_rows[v][:], in_=rec_parts[v])
-            if j == 2:
+            if gate_of(t) == 1:
+                rec_rows[part_of(t)] = keep.tile([P, GATES, BANK], BF16, name="rec_rows%d" % part_of(t))
+                nc.sync.dma_start(out=rec_rows[part_of(t)][:], in_=rec_parts[part_of(t)])
+            if t == GATE_F + 2:
                 nc.sync.dma_start(out=c_rows[:], in_=c_old)
 
         ident_f32 = keep.tile([P, P], F32)
@@ -92,14 +104,16 @@ def tile_yourlstm_pc_kernel(tc, h_below, gates_rec, c_old, w_ih, b_ih, b_hh, out
             in_=h_t[:].rearrange("q s u m -> q s m u"),
         )
 
-        bias_t = psum_bias.tile([P, P], BF16, tag="bias_bank")
-        nc.tensor.transpose(bias_t[:], bias_rows[:], ident_bf16[:])
-        bias_both = keep.tile([P, 2 * bias_blocks], F32)
-        nc.vector.tensor_copy(out=bias_both[:], in_=bias_t[:, 0 : 2 * bias_blocks])
         bias_col = keep.tile([P, bias_blocks], F32)
-        nc.vector.tensor_add(
-            out=bias_col[:], in0=bias_both[:, 0:bias_blocks], in1=bias_both[:, bias_blocks : 2 * bias_blocks]
-        )
+
+        def transpose_biases():
+            bias_t = psum_bias.tile([P, P], BF16, tag="bias_bank")
+            nc.tensor.transpose(bias_t[:], bias_rows[:], ident_bf16[:])
+            bias_both = keep.tile([P, 2 * bias_blocks], F32)
+            nc.vector.tensor_copy(out=bias_both[:], in_=bias_t[:, 0 : 2 * bias_blocks])
+            nc.vector.tensor_add(
+                out=bias_col[:], in0=bias_both[:, 0:bias_blocks], in1=bias_both[:, bias_blocks : 2 * bias_blocks]
+            )
 
         h_codes = keep.tile([P, PASSES * P], U32, align_bytes=64)
         h_scales = keep.tile([P, PASSES * P], U8, align_bytes=64)
@@ -115,143 +129,121 @@ def tile_yourlstm_pc_kernel(tc, h_below, gates_rec, c_old, w_ih, b_ih, b_hh, out
         scales = {}
         products = {}
         gates = {}
-        sig_if = {}
-        tanh_g = {}
+        active = {}
         kept = {}
         fresh = {}
-        sig_o = {}
         tanh_c = {}
 
-        def live(j):
-            return 0 <= j < CHUNKS
-
-        def units(j):
-            return slice(j * P, (j + 1) * P)
-
-        def broadcast_bias(j):
-            bias_banks[j] = psum_bias.tile([P, GATES, P], F32, name="bias_bank", tag="bias_bank")
-            for g in range(GATES):
-                m = g * CHUNKS + j
+        def broadcast_bias(t):
+            bias_banks[t] = psum_bias.tile([P, BANK // P, P], F32, name="bias_bank", tag="bias_bank")
+            for x in range(BANK // P):
+                m = (gate_of(t) * HIDDEN + part_of(t) * BANK) // P + x
                 nc.tensor.transpose(
-                    bias_banks[j][:, g, :], bias_col[:, m : m + 1].to_broadcast([P, P]), ident_f32[:]
+                    bias_banks[t][:, x, :], bias_col[:, m : m + 1].to_broadcast([P, P]), ident_f32[:]
                 )
 
-        def add_bias_to_rec(j):
-            rest[j] = stage.tile([P, GATES, P], F32, name="rest", tag="rest")
+        def add_bias_to_rec(t):
+            rest[t] = stage.tile([P, BANK], F32, name="rest", tag="rest")
             nc.vector.tensor_tensor(
-                out=rest[j][:],
-                in0=bias_banks[j][:],
-                in1=rec_rows[j // REC_CHUNKS][:, :, units(j % REC_CHUNKS)],
+                out=rest[t][:],
+                in0=bias_banks[t][:].rearrange("b x r -> b (x r)"),
+                in1=rec_rows[part_of(t)][:, gate_of(t), :],
                 op=ALU.add,
             )
 
-        def transpose_w(j):
-            for pair in range(PAIRS):
-                words = w_rows[(j, pair)][:].bitcast(F32)
+        def transpose_w(t):
+            for e in range(PIECES):
+                words = w_rows[(t, e)][:].bitcast(F32)
                 for s in range(PASSES):
-                    bank = psum_words.tile([P, PAIR, HALVES, P], F32, name="word_bank", tag="word_bank")
-                    for g2 in range(PAIR):
+                    bank = psum_words.tile([P, TILES, HALVES, P], F32, name="word_bank", tag="word_bank")
+                    for x in range(TILES):
                         for u in range(HALVES):
-                            first = g2 * WORDS + (s * HALVES + u) * P
-                            nc.tensor.transpose(bank[:, g2, u, :], words[:, first : first + P], ident_f32[:])
-                    word_banks[(j, pair, s)] = bank
+                            first = x * WORDS + (s * HALVES + u) * P
+                            nc.tensor.transpose(bank[:, x, u, :], words[:, first : first + P], ident_f32[:])
+                    word_banks[(t, e, s)] = bank
 
-        def regroup(j, pair):
-            grouped[(j, pair)] = quant.tile(
-                [P, PASSES * PAIR * P * PACK], BF16, name="grouped", tag="grouped", align_bytes=64
-            )
-            words = grouped[(j, pair)][:].bitcast(F32)
+        def regroup(t, e):
+            grouped[(t, e)] = quant.tile([P, PASSES * ROWS * PACK], BF16, name="grouped", tag="grouped", align_bytes=64)
+            words = grouped[(t, e)][:].bitcast(F32)
             for s in range(PASSES):
                 nc.scalar.copy(
-                    out=words[:, s * BANK : (s + 1) * BANK].rearrange("q (g r u) -> q g r u", g=PAIR, u=HALVES),
-                    in_=word_banks[(j, pair, s)][:].rearrange("q g u r -> q g r u"),
+                    out=words[:, s * BANK : (s + 1) * BANK].rearrange("q (x r u) -> q x r u", x=TILES, u=HALVES),
+                    in_=word_banks[(t, e, s)][:].rearrange("q x u r -> q x r u"),
                 )
 
-        def quantise(j, pair):
-            codes[(j, pair)] = quant.tile([P, PASSES * PAIR * P], U32, name="codes", tag="codes", align_bytes=64)
-            scales[(j, pair)] = quant.tile([P, PASSES * PAIR * P], U8, name="scales", tag="scales", align_bytes=64)
+        def quantise(t, e):
+            codes[(t, e)] = quant.tile([P, PASSES * ROWS], U32, name="codes", tag="codes", align_bytes=64)
+            scales[(t, e)] = quant.tile([P, PASSES * ROWS], U8, name="scales", tag="scales", align_bytes=64)
             nc.vector.quantize_mx(
-                out=codes[(j, pair)][:].bitcast(FP8X4), scales=scales[(j, pair)][:], in_=grouped[(j, pair)][:]
+                out=codes[(t, e)][:].bitcast(FP8X4), scales=scales[(t, e)][:], in_=grouped[(t, e)][:]
             )
 
-        def multiply(j):
-            products[j] = psum_gates.tile([P, GATES * P], F32, name="product", tag="product")
-            width = PAIR * P
-            for pair in range(PAIRS):
+        def multiply(t):
+            products[t] = psum_gates.tile([P, BANK], F32, name="product", tag="product")
+            for e in range(PIECES):
                 for s in range(PASSES):
                     nc.tensor.matmul_mx(
-                        out=products[j][:, pair * width : (pair + 1) * width],
+                        out=products[t][:, e * ROWS : (e + 1) * ROWS],
                         lhsT=h_codes[:, s * P : (s + 1) * P].bitcast(FP8X4),
                         lhsT_scale=h_scales[:, s * P : (s + 1) * P],
-                        rhs=codes[(j, pair)][:, s * width : (s + 1) * width].bitcast(FP8X4),
-                        rhs_scale=scales[(j, pair)][:, s * width : (s + 1) * width],
+                        rhs=codes[(t, e)][:, s * ROWS : (s + 1) * ROWS].bitcast(FP8X4),
+                        rhs_scale=scales[(t, e)][:, s * ROWS : (s + 1) * ROWS],
                         start=(s == 0),
                         stop=(s == PASSES - 1),
                     )
 
-        def add_rest(j):
-            gates[j] = stage.tile([P, GATES, P], F32, name="gates", tag="gates")
-            nc.vector.tensor_tensor(
-                out=gates[j][:].rearrange("b g r -> b (g r)"),
-                in0=products[j][:],
-                in1=rest[j][:].rearrange("b g r -> b (g r)"),
-                op=ALU.add,
-            )
+        def add_rest(t):
+            gates[t] = stage.tile([P, BANK], F32, name="gates", tag="gates")
+            nc.vector.tensor_tensor(out=gates[t][:], in0=products[t][:], in1=rest[t][:], op=ALU.add)
 
-        def activate_i_f_g(j):
-            sig_if[j] = stage.tile([P, 2, P], F32, name="sig_if", tag="sig_if")
-            nc.scalar.activation(out=sig_if[j][:], in_=gates[j][:, 0:2, :], func=ACT.Sigmoid)
-            tanh_g[j] = stage.tile([P, P], F32, name="tanh_g", tag="tanh_g")
-            nc.scalar.activation(out=tanh_g[j][:], in_=gates[j][:, 2, :], func=ACT.Tanh)
+        def activate(t):
+            active[t] = active_pool.tile([P, BANK], F32, name="active", tag="active")
+            func = ACT.Tanh if gate_of(t) == GATE_G else ACT.Sigmoid
+            nc.scalar.activation(out=active[t][:], in_=gates[t][:], func=func)
 
-        def store(out, result, j):
-            if (j + 1) % STORE_CHUNKS == 0:
-                cols = slice((j + 1 - STORE_CHUNKS) * P, (j + 1) * P)
-                nc.sync.dma_start(out=out[:, cols], in_=result[:, cols])
+        def use_gate(t):
+            part = part_of(t)
+            if gate_of(t) == GATE_F:
+                kept[part] = stage.tile([P, BANK], F32, name="kept", tag="kept")
+                nc.vector.tensor_mul(out=kept[part][:], in0=active[t][:], in1=c_rows[:, units(part)])
+            if gate_of(t) == GATE_G:
+                fresh[part] = stage.tile([P, BANK], F32, name="fresh", tag="fresh")
+                nc.vector.tensor_mul(out=fresh[part][:], in0=active[t - GATE_G][:], in1=active[t][:])
+            if gate_of(t) == GATE_O:
+                nc.vector.tensor_mul(out=h_new[:, units(part)], in0=active[t][:], in1=tanh_c[part][:])
+                nc.sync.dma_start(out=out_0[:, units(part)], in_=h_new[:, units(part)])
 
-        def gate_cell(j):
-            kept[j] = stage.tile([P, P], F32, name="kept", tag="kept")
-            nc.vector.tensor_mul(out=kept[j][:], in0=sig_if[j][:, 1, :], in1=c_rows[:, units(j)])
-            fresh[j] = stage.tile([P, P], F32, name="fresh", tag="fresh")
-            nc.vector.tensor_mul(out=fresh[j][:], in0=sig_if[j][:, 0, :], in1=tanh_g[j][:])
+        def update_cell(part):
+            nc.vector.tensor_add(out=c_new[:, units(part)], in0=kept[part][:], in1=fresh[part][:])
+            nc.sync.dma_start(out=out_1[:, units(part)], in_=c_new[:, units(part)])
 
-        def update_cell(j):
-            nc.vector.tensor_add(out=c_new[:, units(j)], in0=kept[j][:], in1=fresh[j][:])
-            store(out_1, c_new, j)
+        def activate_cell(part):
+            tanh_c[part] = stage.tile([P, BANK], F32, name="tanh_c", tag="tanh_c")
+            nc.scalar.activation(out=tanh_c[part][:], in_=c_new[:, units(part)], func=ACT.Tanh)
 
-        def activate_o_c(j):
-            sig_o[j] = stage.tile([P, P], F32, name="sig_o", tag="sig_o")
-            nc.scalar.activation(out=sig_o[j][:], in_=gates[j][:, 3, :], func=ACT.Sigmoid)
-            tanh_c[j] = stage.tile([P, P], F32, name="tanh_c", tag="tanh_c")
-            nc.scalar.activation(out=tanh_c[j][:], in_=c_new[:, units(j)], func=ACT.Tanh)
-
-        def update_hidden(j):
-            nc.vector.tensor_mul(out=h_new[:, units(j)], in0=sig_o[j][:], in1=tanh_c[j][:])
-            store(out_0, h_new, j)
-
-        for t in range(CHUNKS + 2):
-            if live(t - 1):
-                broadcast_bias(t - 1)
+        for t in range(SLABS + 2):
+            used = gate_of(t - 2) if live(t - 2) else None
             if live(t):
                 transpose_w(t)
             if live(t - 1):
+                broadcast_bias(t - 1)
                 multiply(t - 1)
-            if live(t - 2):
-                activate_i_f_g(t - 2)
-                gate_cell(t - 2)
-            if live(t - 1):
-                add_bias_to_rec(t - 1)
             if live(t):
                 regroup(t, 0)
+                quantise(t, 0)
+            if live(t - 1):
+                add_bias_to_rec(t - 1)
+            if used == GATE_O:
+                activate_cell(part_of(t - 2))
             if live(t - 2):
-                update_cell(t - 2)
-                activate_o_c(t - 2)
+                activate(t - 2)
+                use_gate(t - 2)
+            if used == GATE_G:
+                update_cell(part_of(t - 2))
             if live(t - 1):
                 add_rest(t - 1)
             if live(t):
-                quantise(t, 0)
                 regroup(t, 1)
-            if live(t - 2):
-                update_hidden(t - 2)
-            if live(t):
                 quantise(t, 1)
+            if t == 0:
+                transpose_biases()

from contextlib import ExitStack

import concourse.mybir as mybir
from concourse.masks import make_identity

F32 = mybir.dt.float32
BF16 = mybir.dt.bfloat16
U32 = mybir.dt.uint32
U8 = mybir.dt.uint8
FP8X4 = mybir.dt.float8_e4m3fn_x4
ACT = mybir.ActivationFunctionType
ALU = mybir.AluOpType

P = 128
FEATURES = 1024
HIDDEN = 1024
GATES = 4
GATE_F, GATE_G, GATE_O = 1, 2, 3
PACK = 4
PASSES = FEATURES // (P * PACK)
HALVES = 2
WORDS = FEATURES // 2
BANK = 512
PARTS = HIDDEN // BANK
SLABS = PARTS * GATES
PIECES = 2
ROWS = BANK // PIECES
TILES = ROWS // P

FLOPS = 2 * P * FEATURES * GATES * HIDDEN


def tile_yourlstm_pc_kernel(tc, h_below, gates_rec, c_old, w_ih, b_ih, b_hh, out_0, out_1):
    nc = tc.nc
    with ExitStack() as ctx:
        keep = ctx.enter_context(tc.tile_pool(name="keep", bufs=1))
        w_pool = ctx.enter_context(tc.tile_pool(name="w", bufs=SLABS * PIECES))
        quant = ctx.enter_context(tc.tile_pool(name="quant", bufs=2 * PIECES))
        stage = ctx.enter_context(tc.tile_pool(name="stage", bufs=2))
        active_pool = ctx.enter_context(tc.tile_pool(name="active", bufs=GATES))
        psum_words = ctx.enter_context(tc.psum_pool(name="psum_words", bufs=3 * PASSES))
        psum_gates = ctx.enter_context(tc.psum_pool(name="psum_gates", bufs=1))
        psum_bias = ctx.enter_context(tc.psum_pool(name="psum_bias", bufs=1))
        ctx.enter_context(tc.manual_schedule())

        def gate_of(t):
            return t % GATES

        def part_of(t):
            return t // GATES

        def live(t):
            return 0 <= t < SLABS

        def units(part):
            return slice(part * BANK, (part + 1) * BANK)

        bias_blocks = GATES * HIDDEN // P
        bias_rows = keep.tile([P, P], BF16)
        nc.vector.memset(bias_rows[2 * bias_blocks : P, :], 0.0)
        nc.scalar.dma_start(out=bias_rows[0:bias_blocks, :], in_=b_ih.rearrange("(m r) -> m r", r=P))
        nc.scalar.dma_start(
            out=bias_rows[bias_blocks : 2 * bias_blocks, :], in_=b_hh.rearrange("(m r) -> m r", r=P)
        )

        h_rows = keep.tile([P, FEATURES], BF16)
        nc.sync.dma_start(out=h_rows[:], in_=h_below)
        w_pieces = w_ih.rearrange("(g v e x r) k -> g v e r x k", g=GATES, v=PARTS, e=PIECES, r=P)
        rec_parts = gates_rec.rearrange("b (g v y) -> v b g y", g=GATES, v=PARTS)
        w_rows = {}
        rec_rows = {}
        c_rows = keep.tile([P, HIDDEN], BF16)
        for t in range(SLABS):
            for e in range(PIECES):
                w_rows[(t, e)] = w_pool.tile([P, TILES * FEATURES], BF16, name="w_rows", tag="w_rows")
                nc.sync.dma_start(
                    out=w_rows[(t, e)][:].rearrange("r (x k) -> r x k", x=TILES),
                    in_=w_pieces[gate_of(t), part_of(t), e],
                )
            if gate_of(t) == 1:
                rec_rows[part_of(t)] = keep.tile([P, GATES, BANK], BF16, name="rec_rows%d" % part_of(t))
                nc.sync.dma_start(out=rec_rows[part_of(t)][:], in_=rec_parts[part_of(t)])
            if t == GATE_F + 2:
                nc.sync.dma_start(out=c_rows[:], in_=c_old)

        ident_f32 = keep.tile([P, P], F32)
        make_identity(nc, ident_f32[:])
        ident_bf16 = keep.tile([P, P], BF16)
        nc.vector.tensor_copy(out=ident_bf16[:], in_=ident_f32[:])
        warm = keep.tile([P, 1], F32)
        nc.vector.memset(warm[:], 0.0)
        warm_out = keep.tile([P, 1], F32)
        nc.scalar.activation(out=warm_out[:], in_=warm[:], func=ACT.Sigmoid)

        h_words = h_rows[:].bitcast(F32)
        h_t = psum_bias.tile([P, PASSES, HALVES, P], F32, tag="bias_bank")
        for s in range(PASSES):
            for u in range(HALVES):
                first = (s * HALVES + u) * P
                nc.tensor.transpose(h_t[:, s, u, :], h_words[:, first : first + P], ident_f32[:])
        h_grouped = keep.tile([P, PASSES * P * PACK], BF16, align_bytes=64)
        nc.vector.tensor_copy(
            out=h_grouped[:].bitcast(F32).rearrange("q (s m u) -> q s m u", s=PASSES, u=HALVES),
            in_=h_t[:].rearrange("q s u m -> q s m u"),
        )

        bias_col = keep.tile([P, bias_blocks], F32)

        def transpose_biases():
            bias_t = psum_bias.tile([P, P], BF16, tag="bias_bank")
            nc.tensor.transpose(bias_t[:], bias_rows[:], ident_bf16[:])
            bias_both = keep.tile([P, 2 * bias_blocks], F32)
            nc.vector.tensor_copy(out=bias_both[:], in_=bias_t[:, 0 : 2 * bias_blocks])
            nc.vector.tensor_add(
                out=bias_col[:], in0=bias_both[:, 0:bias_blocks], in1=bias_both[:, bias_blocks : 2 * bias_blocks]
            )

        h_codes = keep.tile([P, PASSES * P], U32, align_bytes=64)
        h_scales = keep.tile([P, PASSES * P], U8, align_bytes=64)
        nc.vector.quantize_mx(out=h_codes[:].bitcast(FP8X4), scales=h_scales[:], in_=h_grouped[:])

        c_new = keep.tile([P, HIDDEN], F32)
        h_new = keep.tile([P, HIDDEN], F32)
        bias_banks = {}
        rest = {}
        word_banks = {}
        grouped = {}
        codes = {}
        scales = {}
        products = {}
        gates = {}
        active = {}
        kept = {}
        fresh = {}
        tanh_c = {}

        def broadcast_bias(t):
            bias_banks[t] = psum_bias.tile([P, BANK // P, P], F32, name="bias_bank", tag="bias_bank")
            for x in range(BANK // P):
                m = (gate_of(t) * HIDDEN + part_of(t) * BANK) // P + x
                nc.tensor.transpose(
                    bias_banks[t][:, x, :], bias_col[:, m : m + 1].to_broadcast([P, P]), ident_f32[:]
                )

        def add_bias_to_rec(t):
            rest[t] = stage.tile([P, BANK], F32, name="rest", tag="rest")
            nc.vector.tensor_tensor(
                out=rest[t][:],
                in0=bias_banks[t][:].rearrange("b x r -> b (x r)"),
                in1=rec_rows[part_of(t)][:, gate_of(t), :],
                op=ALU.add,
            )

        def transpose_w(t):
            for e in range(PIECES):
                words = w_rows[(t, e)][:].bitcast(F32)
                for s in range(PASSES):
                    bank = psum_words.tile([P, TILES, HALVES, P], F32, name="word_bank", tag="word_bank")
                    for x in range(TILES):
                        for u in range(HALVES):
                            first = x * WORDS + (s * HALVES + u) * P
                            nc.tensor.transpose(bank[:, x, u, :], words[:, first : first + P], ident_f32[:])
                    word_banks[(t, e, s)] = bank

        def regroup(t, e):
            grouped[(t, e)] = quant.tile([P, PASSES * ROWS * PACK], BF16, name="grouped", tag="grouped", align_bytes=64)
            words = grouped[(t, e)][:].bitcast(F32)
            for s in range(PASSES):
                nc.scalar.copy(
                    out=words[:, s * BANK : (s + 1) * BANK].rearrange("q (x r u) -> q x r u", x=TILES, u=HALVES),
                    in_=word_banks[(t, e, s)][:].rearrange("q x u r -> q x r u"),
                )

        def quantise(t, e):
            codes[(t, e)] = quant.tile([P, PASSES * ROWS], U32, name="codes", tag="codes", align_bytes=64)
            scales[(t, e)] = quant.tile([P, PASSES * ROWS], U8, name="scales", tag="scales", align_bytes=64)
            nc.vector.quantize_mx(
                out=codes[(t, e)][:].bitcast(FP8X4), scales=scales[(t, e)][:], in_=grouped[(t, e)][:]
            )

        def multiply(t):
            products[t] = psum_gates.tile([P, BANK], F32, name="product", tag="product")
            for e in range(PIECES):
                for s in range(PASSES):
                    nc.tensor.matmul_mx(
                        out=products[t][:, e * ROWS : (e + 1) * ROWS],
                        lhsT=h_codes[:, s * P : (s + 1) * P].bitcast(FP8X4),
                        lhsT_scale=h_scales[:, s * P : (s + 1) * P],
                        rhs=codes[(t, e)][:, s * ROWS : (s + 1) * ROWS].bitcast(FP8X4),
                        rhs_scale=scales[(t, e)][:, s * ROWS : (s + 1) * ROWS],
                        start=(s == 0),
                        stop=(s == PASSES - 1),
                    )

        def add_rest(t):
            gates[t] = stage.tile([P, BANK], F32, name="gates", tag="gates")
            nc.vector.tensor_tensor(out=gates[t][:], in0=products[t][:], in1=rest[t][:], op=ALU.add)

        def activate(t):
            active[t] = active_pool.tile([P, BANK], F32, name="active", tag="active")
            func = ACT.Tanh if gate_of(t) == GATE_G else ACT.Sigmoid
            nc.scalar.activation(out=active[t][:], in_=gates[t][:], func=func)

        def use_gate(t):
            part = part_of(t)
            if gate_of(t) == GATE_F:
                kept[part] = stage.tile([P, BANK], F32, name="kept", tag="kept")
                nc.vector.tensor_mul(out=kept[part][:], in0=active[t][:], in1=c_rows[:, units(part)])
            if gate_of(t) == GATE_G:
                fresh[part] = stage.tile([P, BANK], F32, name="fresh", tag="fresh")
                nc.vector.tensor_mul(out=fresh[part][:], in0=active[t - GATE_G][:], in1=active[t][:])
            if gate_of(t) == GATE_O:
                nc.vector.tensor_mul(out=h_new[:, units(part)], in0=active[t][:], in1=tanh_c[part][:])
                nc.sync.dma_start(out=out_0[:, units(part)], in_=h_new[:, units(part)])

        def update_cell(part):
            nc.vector.tensor_add(out=c_new[:, units(part)], in0=kept[part][:], in1=fresh[part][:])
            nc.sync.dma_start(out=out_1[:, units(part)], in_=c_new[:, units(part)])

        def activate_cell(part):
            tanh_c[part] = stage.tile([P, BANK], F32, name="tanh_c", tag="tanh_c")
            nc.scalar.activation(out=tanh_c[part][:], in_=c_new[:, units(part)], func=ACT.Tanh)

        for t in range(SLABS + 2):
            used = gate_of(t - 2) if live(t - 2) else None
            if live(t):
                transpose_w(t)
            if live(t - 1):
                broadcast_bias(t - 1)
                multiply(t - 1)
            if live(t):
                regroup(t, 0)
                quantise(t, 0)
            if live(t - 1):
                add_bias_to_rec(t - 1)
            if used == GATE_O:
                activate_cell(part_of(t - 2))
            if live(t - 2):
                activate(t - 2)
                use_gate(t - 2)
            if used == GATE_G:
                update_cell(part_of(t - 2))
            if live(t - 1):
                add_rest(t - 1)
            if live(t):
                regroup(t, 1)
                quantise(t, 1)
            if t == 0:
                transpose_biases()
